import numpy as np
import ml_dtypes

BF16 = ml_dtypes.bfloat16


def bf(x):
    return np.asarray(x, np.float32).astype(BF16)


def f32(x):
    return np.asarray(x, np.float32)


def f64(x):
    return np.asarray(x).astype(np.float64)


def striped(idx):
    return np.tile(idx.reshape(-1, 16).T, (8, 1))


C, S, N = 512, 2048, 1024


def setup_inputs():
    return {"token_emb": f32(np.random.standard_normal((C, S))), "pos_emb": f32(np.random.standard_normal((C, N))), "gamma": f32(0.1 * np.random.standard_normal((C, 1))), "offs": striped(np.random.permutation(np.tile(np.arange(S), 2))[:N])}


def reference(token_emb, pos_emb, gamma, offs):
    idx = offs[:16].T.reshape(-1)
    x = f64(token_emb)[:, idx] + f64(pos_emb)
    r = np.sqrt(np.sum(x * x, axis=0, keepdims=True))
    return x / r * np.sqrt(C) * (f64(gamma) + 1.0)

@@ -1,0 +1,64 @@
+import concourse.mybir as mybir
+
+P = 128
+C, S, N = 512, 2048, 1024
+BLOCKS = C // P
+BANK = 512
+HALVES = N // BANK
+
+F32 = mybir.dt.float32
+U16 = mybir.dt.uint16
+ADD = mybir.AluOpType.add
+MULT = mybir.AluOpType.mult
+SQUARE = mybir.ActivationFunctionType.Square
+RSQRT = mybir.ActivationFunctionType.Abs_reciprocal_sqrt
+
+
+def tile_l2distancetransformer_kernel(tc, token_emb, pos_emb, gamma, offs, out):
+    nc = tc.nc
+    with (
+        tc.tile_pool(name="held", bufs=1) as held,
+        tc.tile_pool(name="ring", bufs=2) as ring,
+        tc.psum_pool(name="psum", bufs=1) as psum,
+    ):
+        offsets = held.tile([P, N // 16], U16, name="offsets")
+        nc.sync.dma_start(offsets[:], offs)
+
+        gamma_cols = held.tile([P, BLOCKS], F32, name="gamma_cols")
+        with nc.allow_non_contiguous_dma(reason="512 single floats, one to a partition and block"):
+            nc.scalar.dma_start(gamma_cols[:], gamma.rearrange("(b p) o -> p (b o)", p=P))
+        gain = held.tile([P, BLOCKS], F32, name="gain")
+        nc.vector.tensor_scalar_add(gain[:], gamma_cols[:], 1.0)
+
+        mean_weights = held.tile([P, P], F32, name="mean_weights")
+        nc.gpsimd.memset(mean_weights[:], 1.0 / C)
+
+        tables = [held.tile([P, S], F32, name=f"table{b}") for b in range(BLOCKS)]
+        positions = [held.tile([P, N], F32, name=f"position{b}") for b in range(BLOCKS)]
+        for b in range(BLOCKS):
+            nc.sync.dma_start(tables[b][:], token_emb[b * P : (b + 1) * P, :])
+            nc.sync.dma_start(positions[b][:], pos_emb[b * P : (b + 1) * P, :])
+
+        mean_square = [psum.tile([P, BANK], F32, name=f"mean_square{h}") for h in range(HALVES)]
+        xs = [held.tile([P, N], F32, name=f"x{b}") for b in range(BLOCKS)]
+        for b in range(BLOCKS):
+            nc.vector.tensor_tensor(xs[b][:], tables[b][:].indirect(offsets[:]), positions[b][:], ADD)
+            squares = ring.tile([P, N], F32, name="squares")
+            nc.scalar.activation(squares[:], xs[b][:], SQUARE)
+            for h in range(HALVES):
+                nc.tensor.matmul(
+                    mean_square[h][:],
+                    mean_weights[:],
+                    squares[:, h * BANK : (h + 1) * BANK],
+                    start=(b == 0),
+                    stop=(b == BLOCKS - 1),
+                )
+
+        inv_rms = held.tile([P, N], F32, name="inv_rms")
+        for h in range(HALVES):
+            nc.scalar.activation(inv_rms[:, h * BANK : (h + 1) * BANK], mean_square[h][:], RSQRT)
+
+        for b in range(BLOCKS):
+            normed = ring.tile([P, N], F32, name="normed")
+            nc.vector.scalar_tensor_tensor(normed[:], xs[b][:], gain[:, b : b + 1], inv_rms[:], MULT, MULT)
+            nc.sync.dma_start(out[b * P : (b + 1) * P, :], normed[:])

@@ -3,8 +3,8 @@ import concourse.mybir as mybir
 P = 128
 C, S, N = 512, 2048, 1024
 BLOCKS = C // P
-BANK = 512
-HALVES = N // BANK
+PIECE = 256
+PIECES = N // PIECE
 
 F32 = mybir.dt.float32
 U16 = mybir.dt.uint16
@@ -18,11 +18,17 @@ def tile_l2distancetransformer_kernel(tc, token_emb, pos_emb, gamma, offs, out):
     nc = tc.nc
     with (
         tc.tile_pool(name="held", bufs=1) as held,
-        tc.tile_pool(name="ring", bufs=2) as ring,
+        tc.tile_pool(name="ring", bufs=4) as ring,
         tc.psum_pool(name="psum", bufs=1) as psum,
     ):
         offsets = held.tile([P, N // 16], U16, name="offsets")
         nc.sync.dma_start(offsets[:], offs)
+
+        tables = [held.tile([P, S], F32, name=f"table{b}") for b in range(BLOCKS)]
+        positions = [held.tile([P, N], F32, name=f"position{b}") for b in range(BLOCKS)]
+        for b in range(BLOCKS):
+            nc.sync.dma_start(tables[b][:], token_emb[b * P : (b + 1) * P, :])
+            nc.sync.dma_start(positions[b][:], pos_emb[b * P : (b + 1) * P, :])
 
         gamma_cols = held.tile([P, BLOCKS], F32, name="gamma_cols")
         with nc.allow_non_contiguous_dma(reason="512 single floats, one to a partition and block"):
@@ -33,32 +39,31 @@ def tile_l2distancetransformer_kernel(tc, token_emb, pos_emb, gamma, offs, out):
         mean_weights = held.tile([P, P], F32, name="mean_weights")
         nc.gpsimd.memset(mean_weights[:], 1.0 / C)
 
-        tables = [held.tile([P, S], F32, name=f"table{b}") for b in range(BLOCKS)]
-        positions = [held.tile([P, N], F32, name=f"position{b}") for b in range(BLOCKS)]
-        for b in range(BLOCKS):
-            nc.sync.dma_start(tables[b][:], token_emb[b * P : (b + 1) * P, :])
-            nc.sync.dma_start(positions[b][:], pos_emb[b * P : (b + 1) * P, :])
+        warm = held.tile([P, 1], F32, name="warm")
+        nc.scalar.activation(warm[:], mean_weights[:, 0:1], RSQRT)
 
-        mean_square = [psum.tile([P, BANK], F32, name=f"mean_square{h}") for h in range(HALVES)]
+        mean_square = [psum.tile([P, PIECE], F32, name=f"mean_square{k}") for k in range(PIECES)]
         xs = [held.tile([P, N], F32, name=f"x{b}") for b in range(BLOCKS)]
         for b in range(BLOCKS):
-            nc.vector.tensor_tensor(xs[b][:], tables[b][:].indirect(offsets[:]), positions[b][:], ADD)
-            squares = ring.tile([P, N], F32, name="squares")
-            nc.scalar.activation(squares[:], xs[b][:], SQUARE)
-            for h in range(HALVES):
+            for k in range(PIECES):
+                cols = slice(k * PIECE, (k + 1) * PIECE)
+                piece_offsets = offsets[:, k * (PIECE // 16) : (k + 1) * (PIECE // 16)]
+                nc.vector.tensor_tensor(
+                    xs[b][:, cols], tables[b][:].indirect(piece_offsets), positions[b][:, cols], ADD
+                )
+                squares = ring.tile([P, PIECE], F32, name="squares")
+                nc.scalar.activation(squares[:], xs[b][:, cols], SQUARE)
                 nc.tensor.matmul(
-                    mean_square[h][:],
-                    mean_weights[:],
-                    squares[:, h * BANK : (h + 1) * BANK],
-                    start=(b == 0),
-                    stop=(b == BLOCKS - 1),
+                    mean_square[k][:], mean_weights[:], squares[:], start=(b == 0), stop=(b == BLOCKS - 1)
                 )
 
-        inv_rms = held.tile([P, N], F32, name="inv_rms")
-        for h in range(HALVES):
-            nc.scalar.activation(inv_rms[:, h * BANK : (h + 1) * BANK], mean_square[h][:], RSQRT)
-
-        for b in range(BLOCKS):
-            normed = ring.tile([P, N], F32, name="normed")
-            nc.vector.scalar_tensor_tensor(normed[:], xs[b][:], gain[:, b : b + 1], inv_rms[:], MULT, MULT)
-            nc.sync.dma_start(out[b * P : (b + 1) * P, :], normed[:])
+        normed = [held.tile([P, N], F32, name=f"normed{b}") for b in range(BLOCKS)]
+        for k in range(PIECES):
+            cols = slice(k * PIECE, (k + 1) * PIECE)
+            inv_rms = ring.tile([P, PIECE], F32, name="inv_rms")
+            nc.scalar.activation(inv_rms[:], mean_square[k][:], RSQRT)
+            for b in range(BLOCKS):
+                nc.vector.scalar_tensor_tensor(
+                    normed[b][:, cols], xs[b][:, cols], gain[:, b : b + 1], inv_rms[:], MULT, MULT
+                )
+                nc.sync.dma_start(out[b * P : (b + 1) * P, cols], normed[b][:, cols])

@@ -28,7 +28,9 @@ def tile_l2distancetransformer_kernel(tc, token_emb, pos_emb, gamma, offs, out):
         positions = [held.tile([P, N], F32, name=f"position{b}") for b in range(BLOCKS)]
         for b in range(BLOCKS):
             nc.sync.dma_start(tables[b][:], token_emb[b * P : (b + 1) * P, :])
-            nc.sync.dma_start(positions[b][:], pos_emb[b * P : (b + 1) * P, :])
+            for k in range(PIECES):
+                cols = slice(k * PIECE, (k + 1) * PIECE)
+                nc.sync.dma_start(positions[b][:, cols], pos_emb[b * P : (b + 1) * P, cols])
 
         gamma_cols = held.tile([P, BLOCKS], F32, name="gamma_cols")
         with nc.allow_non_contiguous_dma(reason="512 single floats, one to a partition and block"):

@@ -34,9 +34,9 @@ def tile_l2distancetransformer_kernel(tc, token_emb, pos_emb, gamma, offs, out):
 
         gamma_cols = held.tile([P, BLOCKS], F32, name="gamma_cols")
         with nc.allow_non_contiguous_dma(reason="512 single floats, one to a partition and block"):
-            nc.scalar.dma_start(gamma_cols[:], gamma.rearrange("(b p) o -> p (b o)", p=P))
+            nc.sync.dma_start(gamma_cols[:], gamma.rearrange("(b p) o -> p (b o)", p=P))
         gain = held.tile([P, BLOCKS], F32, name="gain")
-        nc.vector.tensor_scalar_add(gain[:], gamma_cols[:], 1.0)
+        nc.gpsimd.tensor_scalar_add(gain[:], gamma_cols[:], 1.0)
 
         mean_weights = held.tile([P, P], F32, name="mean_weights")
         nc.gpsimd.memset(mean_weights[:], 1.0 / C)

@@ -5,6 +5,7 @@ C, S, N = 512, 2048, 1024
 BLOCKS = C // P
 PIECE = 256
 PIECES = N // PIECE
+STORE_GROUPS = [[0], [1], [2, 3]]
 
 F32 = mybir.dt.float32
 U16 = mybir.dt.uint16
@@ -60,12 +61,16 @@ def tile_l2distancetransformer_kernel(tc, token_emb, pos_emb, gamma, offs, out):
                 )
 
         normed = [held.tile([P, N], F32, name=f"normed{b}") for b in range(BLOCKS)]
-        for k in range(PIECES):
-            cols = slice(k * PIECE, (k + 1) * PIECE)
-            inv_rms = ring.tile([P, PIECE], F32, name="inv_rms")
-            nc.scalar.activation(inv_rms[:], mean_square[k][:], RSQRT)
+        for group in STORE_GROUPS:
+            inv_rms = {}
+            for k in group:
+                inv_rms[k] = ring.tile([P, PIECE], F32, name="inv_rms")
+                nc.scalar.activation(inv_rms[k][:], mean_square[k][:], RSQRT)
+            span = slice(group[0] * PIECE, (group[-1] + 1) * PIECE)
             for b in range(BLOCKS):
-                nc.vector.scalar_tensor_tensor(
-                    normed[b][:, cols], xs[b][:, cols], gain[:, b : b + 1], inv_rms[:], MULT, MULT
-                )
-                nc.sync.dma_start(out[b * P : (b + 1) * P, cols], normed[b][:, cols])
+                for k in group:
+                    cols = slice(k * PIECE, (k + 1) * PIECE)
+                    nc.vector.scalar_tensor_tensor(
+                        normed[b][:, cols], xs[b][:, cols], gain[:, b : b + 1], inv_rms[k][:], MULT, MULT
+                    )
+                nc.sync.dma_start(out[b * P : (b + 1) * P, span], normed[b][:, span])

@@ -3,9 +3,13 @@ import concourse.mybir as mybir
 P = 128
 C, S, N = 512, 2048, 1024
 BLOCKS = C // P
-PIECE = 256
-PIECES = N // PIECE
-STORE_GROUPS = [[0], [1], [2, 3]]
+CHUNK = 256
+CHUNKS = N // CHUNK
+WIDTHS = [128, 128, 256, 256, 256]
+assert sum(WIDTHS) == N
+STARTS = [sum(WIDTHS[:k]) for k in range(len(WIDTHS))]
+PIECES = len(WIDTHS)
+STORE_GROUPS = [[0, 1], [2], [3, 4]]
 
 F32 = mybir.dt.float32
 U16 = mybir.dt.uint16
@@ -29,8 +33,8 @@ def tile_l2distancetransformer_kernel(tc, token_emb, pos_emb, gamma, offs, out):
         positions = [held.tile([P, N], F32, name=f"position{b}") for b in range(BLOCKS)]
         for b in range(BLOCKS):
             nc.sync.dma_start(tables[b][:], token_emb[b * P : (b + 1) * P, :])
-            for k in range(PIECES):
-                cols = slice(k * PIECE, (k + 1) * PIECE)
+            for h in range(CHUNKS):
+                cols = slice(h * CHUNK, (h + 1) * CHUNK)
                 nc.sync.dma_start(positions[b][:, cols], pos_emb[b * P : (b + 1) * P, cols])
 
         gamma_cols = held.tile([P, BLOCKS], F32, name="gamma_cols")
@@ -45,32 +49,40 @@ def tile_l2distancetransformer_kernel(tc, token_emb, pos_emb, gamma, offs, out):
         warm = held.tile([P, 1], F32, name="warm")
         nc.scalar.activation(warm[:], mean_weights[:, 0:1], RSQRT)
 
-        mean_square = [psum.tile([P, PIECE], F32, name=f"mean_square{k}") for k in range(PIECES)]
+        mean_square = [psum.tile([P, WIDTHS[k]], F32, name=f"mean_square{k}") for k in range(PIECES)]
         xs = [held.tile([P, N], F32, name=f"x{b}") for b in range(BLOCKS)]
         for b in range(BLOCKS):
             for k in range(PIECES):
-                cols = slice(k * PIECE, (k + 1) * PIECE)
-                piece_offsets = offsets[:, k * (PIECE // 16) : (k + 1) * (PIECE // 16)]
+                cols = slice(STARTS[k], STARTS[k] + WIDTHS[k])
+                piece_offsets = offsets[:, cols.start // 16 : cols.stop // 16]
                 nc.vector.tensor_tensor(
                     xs[b][:, cols], tables[b][:].indirect(piece_offsets), positions[b][:, cols], ADD
                 )
-                squares = ring.tile([P, PIECE], F32, name="squares")
-                nc.scalar.activation(squares[:], xs[b][:, cols], SQUARE)
+                squares = ring.tile([P, CHUNK], F32, name="squares")
+                nc.scalar.activation(squares[:, : WIDTHS[k]], xs[b][:, cols], SQUARE)
                 nc.tensor.matmul(
-                    mean_square[k][:], mean_weights[:], squares[:], start=(b == 0), stop=(b == BLOCKS - 1)
+                    mean_square[k][:],
+                    mean_weights[:],
+                    squares[:, : WIDTHS[k]],
+                    start=(b == 0),
+                    stop=(b == BLOCKS - 1),
                 )
 
         normed = [held.tile([P, N], F32, name=f"normed{b}") for b in range(BLOCKS)]
         for group in STORE_GROUPS:
             inv_rms = {}
             for k in group:
-                inv_rms[k] = ring.tile([P, PIECE], F32, name="inv_rms")
-                nc.scalar.activation(inv_rms[k][:], mean_square[k][:], RSQRT)
-            span = slice(group[0] * PIECE, (group[-1] + 1) * PIECE)
+                inv_rms[k] = ring.tile([P, CHUNK], F32, name="inv_rms")
+                nc.scalar.activation(inv_rms[k][:, : WIDTHS[k]], mean_square[k][:], RSQRT)
+            span = slice(STARTS[group[0]], STARTS[group[-1]] + WIDTHS[group[-1]])
             for b in range(BLOCKS):
+                one_by_one = group == STORE_GROUPS[-1] and b == BLOCKS - 1
                 for k in group:
-                    cols = slice(k * PIECE, (k + 1) * PIECE)
+                    cols = slice(STARTS[k], STARTS[k] + WIDTHS[k])
                     nc.vector.scalar_tensor_tensor(
-                        normed[b][:, cols], xs[b][:, cols], gain[:, b : b + 1], inv_rms[k][:], MULT, MULT
+                        normed[b][:, cols], xs[b][:, cols], gain[:, b : b + 1], inv_rms[k][:, : WIDTHS[k]], MULT, MULT
                     )
-                nc.sync.dma_start(out[b * P : (b + 1) * P, span], normed[b][:, span])
+                    if one_by_one:
+                        nc.sync.dma_start(out[b * P : (b + 1) * P, cols], normed[b][:, cols])
+                if not one_by_one:
+                    nc.sync.dma_start(out[b * P : (b + 1) * P, span], normed[b][:, span])

import concourse.mybir as mybir

P = 128
C, S, N = 512, 2048, 1024
BLOCKS = C // P
CHUNK = 256
CHUNKS = N // CHUNK
WIDTHS = [128, 128, 256, 256, 256]
assert sum(WIDTHS) == N
STARTS = [sum(WIDTHS[:k]) for k in range(len(WIDTHS))]
PIECES = len(WIDTHS)
STORE_GROUPS = [[0, 1], [2], [3, 4]]

F32 = mybir.dt.float32
U16 = mybir.dt.uint16
ADD = mybir.AluOpType.add
MULT = mybir.AluOpType.mult
SQUARE = mybir.ActivationFunctionType.Square
RSQRT = mybir.ActivationFunctionType.Abs_reciprocal_sqrt


def tile_l2distancetransformer_kernel(tc, token_emb, pos_emb, gamma, offs, out):
    nc = tc.nc
    with (
        tc.tile_pool(name="held", bufs=1) as held,
        tc.tile_pool(name="ring", bufs=4) as ring,
        tc.psum_pool(name="psum", bufs=1) as psum,
    ):
        offsets = held.tile([P, N // 16], U16, name="offsets")
        nc.sync.dma_start(offsets[:], offs)

        tables = [held.tile([P, S], F32, name=f"table{b}") for b in range(BLOCKS)]
        positions = [held.tile([P, N], F32, name=f"position{b}") for b in range(BLOCKS)]
        for b in range(BLOCKS):
            nc.sync.dma_start(tables[b][:], token_emb[b * P : (b + 1) * P, :])
            for h in range(CHUNKS):
                cols = slice(h * CHUNK, (h + 1) * CHUNK)
                nc.sync.dma_start(positions[b][:, cols], pos_emb[b * P : (b + 1) * P, cols])

        gamma_cols = held.tile([P, BLOCKS], F32, name="gamma_cols")
        with nc.allow_non_contiguous_dma(reason="512 single floats, one to a partition and block"):
            nc.sync.dma_start(gamma_cols[:], gamma.rearrange("(b p) o -> p (b o)", p=P))
        gain = held.tile([P, BLOCKS], F32, name="gain")
        nc.gpsimd.tensor_scalar_add(gain[:], gamma_cols[:], 1.0)

        mean_weights = held.tile([P, P], F32, name="mean_weights")
        nc.gpsimd.memset(mean_weights[:], 1.0 / C)

        warm = held.tile([P, 1], F32, name="warm")
        nc.scalar.activation(warm[:], mean_weights[:, 0:1], RSQRT)

        mean_square = [psum.tile([P, WIDTHS[k]], F32, name=f"mean_square{k}") for k in range(PIECES)]
        xs = [held.tile([P, N], F32, name=f"x{b}") for b in range(BLOCKS)]
        for b in range(BLOCKS):
            for k in range(PIECES):
                cols = slice(STARTS[k], STARTS[k] + WIDTHS[k])
                piece_offsets = offsets[:, cols.start // 16 : cols.stop // 16]
                nc.vector.tensor_tensor(
                    xs[b][:, cols], tables[b][:].indirect(piece_offsets), positions[b][:, cols], ADD
                )
                squares = ring.tile([P, CHUNK], F32, name="squares")
                nc.scalar.activation(squares[:, : WIDTHS[k]], xs[b][:, cols], SQUARE)
                nc.tensor.matmul(
                    mean_square[k][:],
                    mean_weights[:],
                    squares[:, : WIDTHS[k]],
                    start=(b == 0),
                    stop=(b == BLOCKS - 1),
                )

        normed = [held.tile([P, N], F32, name=f"normed{b}") for b in range(BLOCKS)]
        for group in STORE_GROUPS:
            inv_rms = {}
            for k in group:
                inv_rms[k] = ring.tile([P, CHUNK], F32, name="inv_rms")
                nc.scalar.activation(inv_rms[k][:, : WIDTHS[k]], mean_square[k][:], RSQRT)
            span = slice(STARTS[group[0]], STARTS[group[-1]] + WIDTHS[group[-1]])
            for b in range(BLOCKS):
                one_by_one = group == STORE_GROUPS[-1] and b == BLOCKS - 1
                for k in group:
                    cols = slice(STARTS[k], STARTS[k] + WIDTHS[k])
                    nc.vector.scalar_tensor_tensor(
                        normed[b][:, cols], xs[b][:, cols], gain[:, b : b + 1], inv_rms[k][:, : WIDTHS[k]], MULT, MULT
                    )
                    if one_by_one:
                        nc.sync.dma_start(out[b * P : (b + 1) * P, cols], normed[b][:, cols])
                if not one_by_one:
                    nc.sync.dma_start(out[b * P : (b + 1) * P, span], normed[b][:, span])
